import numpy as np
import ml_dtypes


def mxq(x, axis, fmt="e4m3"):
    dtype, down = {"e4m3": (ml_dtypes.float8_e4m3fn, 7), "e5m2": (ml_dtypes.float8_e5m2, 14)}[fmt]
    v = np.moveaxis(np.asarray(x, np.float32).astype(ml_dtypes.bfloat16).astype(np.float64), axis, -1)
    blocks = v.reshape(v.shape[:-1] + (-1, 32))
    amax = np.abs(blocks).max(-1, keepdims=True)
    byte = np.maximum(np.where(amax > 0, np.frexp(amax)[1] - 1 + 127, 0) - down, 1)
    scale = np.exp2(byte - 127.0)
    codes = (blocks / scale).astype(np.float32).astype(dtype).astype(np.float64)
    return np.moveaxis((codes * scale).reshape(v.shape), -1, axis)


WIDE = False


def mx_kscale(k):
    if not WIDE:
        return np.ones(k)
    levels = np.array([10, -10, 5, -5, 0])
    if k % 512:
        return np.exp2(np.random.permutation(np.resize(levels, k // 32))).repeat(32)
    a = np.empty((k // 512, 16))
    for p in range(k // 512):
        a[p, :8] = np.random.permutation(np.resize(levels, 8))
        for g in range(8):
            far = levels[np.abs(levels - a[p, g]) >= 10]
            a[p, g + 8] = far[np.random.randint(len(far))]
    return np.exp2(a.ravel()).repeat(32)


BF16 = ml_dtypes.bfloat16


def bf(x):
    return np.asarray(x, np.float32).astype(BF16)


def f64(x):
    return np.asarray(x).astype(np.float64)


G, GI, GO, B = 32, 32, 32, 4096
K = G * GI
N = G * GO


def block_gain():
    gain = np.ones((N, K))
    for g in range(G):
        gain[g * GO:(g + 1) * GO, g * GI:(g + 1) * GI] = 0.5
    return gain


def setup_inputs():
    s = mx_kscale(K)
    bound = 1.0 / np.sqrt(K)
    W = np.random.uniform(-bound, bound, (N, K)) * block_gain()
    return {"data": bf(np.random.standard_normal((B, K)) * s),
            "W": bf(W / s[None, :]),
            "b": bf(np.random.standard_normal(N) * 0.3)}


def core(data, W, b):
    return (mxq(f64(data), 1, "e4m3") @ mxq(f64(W), 1, "e4m3").T) + f64(b)


def e4m3fn_bytes(y):
    return np.clip(np.asarray(y, np.float64), -448.0, 448.0).astype(np.float32).astype(ml_dtypes.float8_e4m3fn).view(np.uint8)


Y_SCALE = 340.0


def reference(data, W, b):
    out = core(data, W, b)
    return out, e4m3fn_bytes(out * Y_SCALE)

@@ -1,0 +1,195 @@
+from contextlib import ExitStack
+
+import concourse.mybir as mybir
+from concourse.masks import make_identity
+
+TOKENS, K, N = 4096, 1024, 1024
+FLOPS = 2 * TOKENS * K * N
+Y_SCALE = 340.0
+
+F32 = mybir.dt.float32
+BF16 = mybir.dt.bfloat16
+U32 = mybir.dt.uint32
+U8 = mybir.dt.uint8
+FP8X4 = mybir.dt.float8_e4m3fn_x4
+FP8 = mybir.dt.float8_e4m3fn
+COPY = mybir.ActivationFunctionType.Copy
+ADD = mybir.AluOpType.add
+
+P = 128
+GROUPS = 8
+J = 4
+PASSES = 2
+HALVES = 2
+HALF = 512
+WARM_FIRST = 8
+
+
+def tile_groupfc_kernel(tc, data, W, b, out_0, out_1):
+    nc = tc.nc
+    with ExitStack() as ctx:
+        const = ctx.enter_context(tc.tile_pool(name="const", bufs=1))
+        xin = ctx.enter_context(tc.tile_pool(name="xin", bufs=1))
+        xgp = ctx.enter_context(tc.tile_pool(name="xgp", bufs=4))
+        xcp = ctx.enter_context(tc.tile_pool(name="xcp", bufs=2))
+        o0p = ctx.enter_context(tc.tile_pool(name="o0p", bufs=8))
+        o1p = ctx.enter_context(tc.tile_pool(name="o1p", bufs=4))
+        psum = ctx.enter_context(tc.psum_pool(name="psum", bufs=8))
+        ctx.enter_context(tc.manual_schedule())
+
+        x_view = data.rearrange("(g p j) k -> g p j k", p=P, j=J)
+        o0_view = out_0.rearrange("(g p j) n -> g p j n", p=P, j=J)
+        o1_view = out_1.rearrange("(g p j) n -> g p (j n)", p=P, j=J)
+
+        ones = const.tile([P, P], BF16, name="ones", tag="ones")
+        nc.vector.memset(ones[:], 1.0)
+        zeros = const.tile([P, HALF], BF16, name="zeros", tag="zeros")
+        nc.vector.memset(zeros[:], 0.0)
+        brow = const.tile([P, N], BF16, name="brow", tag="brow")
+        nc.vector.memset(brow[:], 0.0)
+        tiny = const.tile([P, 1], F32, name="tiny", tag="tiny")
+        nc.vector.memset(tiny[:], 0.0)
+        tiny2 = const.tile([P, 1], F32, name="tiny2", tag="tiny2")
+        nc.scalar.activation(out=tiny2[:], in_=tiny[:], func=COPY, scale=Y_SCALE)
+        ident = const.tile([P, P], F32, name="ident", tag="ident")
+        make_identity(nc, ident[:])
+        bias = const.tile([P, N], F32, name="bias", tag="bias")
+
+        w_raw = []
+        for q in range(4):
+            w_raw.append(const.tile([P, 2, K], BF16, name="w_raw%d" % q, tag="w_raw%d" % q))
+        x_tiles = {}
+
+        def load_w(q):
+            nc.sync.dma_start(
+                out=w_raw[q][:],
+                in_=W[256 * q : 256 * (q + 1), :].rearrange("(r p) k -> p r k", p=P),
+            )
+
+        def load_x(g, j0, nj):
+            t = xin.tile([P, nj, K], BF16, name="x%d_%d" % (g, j0), tag="x%d_%d" % (g, j0))
+            nc.sync.dma_start(out=t[:], in_=x_view[g][:, j0 : j0 + nj, :])
+            for j in range(nj):
+                x_tiles[(g, j0 + j)] = t[:, j, :]
+
+        load_w(0)
+        load_w(1)
+        load_x(0, 0, 2)
+        load_x(0, 2, 2)
+        nc.sync.dma_start(out=brow[0:1, :], in_=b.rearrange("(o n) -> o n", o=1))
+        load_w(2)
+        load_w(3)
+        for g in range(1, GROUPS):
+            load_x(g, 0, J)
+
+        def warm(n):
+            wp = psum.tile([P, HALF], F32, name="wp", tag="bank")
+            for i in range(n):
+                nc.tensor.matmul(out=wp[:], lhsT=ones[:], rhs=zeros[:], start=True, stop=True)
+
+        def transposes(src):
+            words = src.bitcast(F32)
+            tp = psum.tile([P, PASSES, 2, P], F32, name="tp", tag="bank")
+            for c in range(PASSES):
+                for u in range(2):
+                    nc.tensor.transpose(
+                        tp[:, c, u, :], words[:, 256 * c + u : 256 * (c + 1) : 2], ident[:]
+                    )
+            return tp
+
+        def copy_out(on_vector, dst_words, tp):
+            src = tp[:].rearrange("p c u r -> p c r u")
+            if on_vector:
+                nc.vector.tensor_copy(out=dst_words, in_=src)
+            else:
+                nc.scalar.copy(out=dst_words, in_=src)
+
+        w_grouped = []
+        for h in range(HALVES):
+            w_grouped.append(
+                const.tile([P, PASSES, HALF, 4], BF16, name="wg%d" % h, tag="wg%d" % h, align_bytes=64)
+            )
+        w_codes = const.tile([P, HALVES, PASSES, HALF], U32, name="w_codes", tag="w_codes", align_bytes=64)
+        w_scales = const.tile([P, HALVES, PASSES, HALF], U8, name="w_scales", tag="w_scales", align_bytes=64)
+
+        def prepare_w(h):
+            for rr in range(4):
+                r = 4 * h + rr
+                tp = transposes(w_raw[r // 2][:, r % 2, :])
+                warm(1)
+                copy_out(rr % 2 == 0, w_grouped[h][:, :, P * rr : P * (rr + 1), :].bitcast(F32), tp)
+            nc.vector.quantize_mx(
+                out=w_codes[:, h].rearrange("p c n -> p (c n)").bitcast(FP8X4),
+                scales=w_scales[:, h].rearrange("p c n -> p (c n)"),
+                in_=w_grouped[h][:].rearrange("p c n t -> p (c n t)"),
+            )
+
+        x_grouped = {}
+        x_codes = {}
+
+        def transpose_x(g, vector_js, warm_each):
+            for a in range(2):
+                xg = xgp.tile([P, 2, PASSES, P, 4], BF16, name="xg", tag="xg", align_bytes=64)
+                x_grouped[(g, a)] = xg
+                for jj in range(2):
+                    j = 2 * a + jj
+                    tp = transposes(x_tiles[(g, j)])
+                    if warm_each:
+                        warm(1)
+                    copy_out(j in vector_js, xg[:, jj].bitcast(F32), tp)
+
+        def quantise_x(g):
+            xc = xcp.tile([P, J, PASSES, P], U32, name="xc", tag="xc", align_bytes=64)
+            xs = xcp.tile([P, J, PASSES, P], U8, name="xs", tag="xs", align_bytes=64)
+            x_codes[g] = (xc, xs)
+            for a in range(2):
+                nc.vector.quantize_mx(
+                    out=xc[:, 2 * a : 2 * a + 2].rearrange("p j c r -> p (j c r)").bitcast(FP8X4),
+                    scales=xs[:, 2 * a : 2 * a + 2].rearrange("p j c r -> p (j c r)"),
+                    in_=x_grouped[(g, a)][:].rearrange("p j c r t -> p (j c r t)"),
+                )
+
+        def multiply(g):
+            xc, xs = x_codes[g]
+            f8 = o1p.tile([P, J, N], FP8, name="f8", tag="f8")
+            for a in range(2):
+                o0 = o0p.tile([P, 2, N], F32, name="o0", tag="o0")
+                for jj in range(2):
+                    j = 2 * a + jj
+                    for h in range(HALVES):
+                        acc = psum.tile([P, HALF], F32, name="acc", tag="bank")
+                        for c in range(PASSES):
+                            nc.tensor.matmul_mx(
+                                out=acc[:],
+                                lhsT=xc[:, j, c, :].bitcast(FP8X4),
+                                lhsT_scale=xs[:, j, c, :],
+                                rhs=w_codes[:, h, c, :].bitcast(FP8X4),
+                                rhs_scale=w_scales[:, h, c, :],
+                                start=(c == 0),
+                                stop=(c == PASSES - 1),
+                            )
+                        cols = slice(HALF * h, HALF * (h + 1))
+                        nc.vector.tensor_tensor(out=o0[:, jj, cols], in0=acc[:], in1=bias[:, cols], op=ADD)
+                    nc.scalar.activation(
+                        out=f8[:, j, :], in_=o0[:, jj, :], func=COPY, scale=Y_SCALE, saturate=False
+                    )
+                nc.sync.dma_start(out=o0_view[g][:, 2 * a : 2 * a + 2, :], in_=o0[:])
+            nc.sync.dma_start(out=o1_view[g], in_=f8[:].rearrange("p j n -> p (j n)").bitcast(U8))
+
+        warm(WARM_FIRST)
+        prepare_w(0)
+        transpose_x(0, (1, 3), True)
+        for h in range(HALVES):
+            bp = psum.tile([P, HALF], F32, name="bp", tag="bank")
+            cols = slice(HALF * h, HALF * (h + 1))
+            nc.tensor.matmul(out=bp[:], lhsT=ones[:], rhs=brow[:, cols], start=True, stop=True)
+            if h == 0:
+                nc.vector.tensor_copy(out=bias[:, cols], in_=bp[:])
+            else:
+                nc.scalar.copy(out=bias[:, cols], in_=bp[:])
+        prepare_w(1)
+        for g in range(GROUPS):
+            quantise_x(g)
+            if g + 1 < GROUPS:
+                transpose_x(g + 1, (3,), False)
+            multiply(g)

@@ -112,11 +112,12 @@ def tile_groupfc_kernel(tc, data, W, b, out_0, out_1):
         w_codes = const.tile([P, HALVES, PASSES, HALF], U32, name="w_codes", tag="w_codes", align_bytes=64)
         w_scales = const.tile([P, HALVES, PASSES, HALF], U8, name="w_scales", tag="w_scales", align_bytes=64)
 
-        def prepare_w(h):
+        def prepare_w(h, warm_each):
             for rr in range(4):
                 r = 4 * h + rr
                 tp = transposes(w_raw[r // 2][:, r % 2, :])
-                warm(1)
+                if warm_each:
+                    warm(1)
                 copy_out(rr % 2 == 0, w_grouped[h][:, :, P * rr : P * (rr + 1), :].bitcast(F32), tp)
             nc.vector.quantize_mx(
                 out=w_codes[:, h].rearrange("p c n -> p (c n)").bitcast(FP8X4),
@@ -149,35 +150,62 @@ def tile_groupfc_kernel(tc, data, W, b, out_0, out_1):
                     in_=x_grouped[(g, a)][:].rearrange("p j c r t -> p (j c r t)"),
                 )
 
-        def multiply(g):
-            xc, xs = x_codes[g]
+        outs = {}
+
+        def store_chunks(g):
+            if g == GROUPS - 1:
+                return ((0, 2), (2, 1), (3, 1)), ((0, 2), (2, 1), (3, 1))
+            return ((0, 2), (2, 2)), ((0, 4),)
+
+        def open_group(g):
             f8 = o1p.tile([P, J, N], FP8, name="f8", tag="f8")
-            for a in range(2):
-                o0 = o0p.tile([P, 2, N], F32, name="o0", tag="o0")
-                for jj in range(2):
-                    j = 2 * a + jj
-                    for h in range(HALVES):
-                        acc = psum.tile([P, HALF], F32, name="acc", tag="bank")
-                        for c in range(PASSES):
-                            nc.tensor.matmul_mx(
-                                out=acc[:],
-                                lhsT=xc[:, j, c, :].bitcast(FP8X4),
-                                lhsT_scale=xs[:, j, c, :],
-                                rhs=w_codes[:, h, c, :].bitcast(FP8X4),
-                                rhs_scale=w_scales[:, h, c, :],
-                                start=(c == 0),
-                                stop=(c == PASSES - 1),
-                            )
-                        cols = slice(HALF * h, HALF * (h + 1))
-                        nc.vector.tensor_tensor(out=o0[:, jj, cols], in0=acc[:], in1=bias[:, cols], op=ADD)
-                    nc.scalar.activation(
-                        out=f8[:, j, :], in_=o0[:, jj, :], func=COPY, scale=Y_SCALE, saturate=False
+            o0a = o0p.tile([P, 2, N], F32, name="o0", tag="o0")
+            o0b = o0p.tile([P, 2, N], F32, name="o0", tag="o0")
+            outs[g] = (f8, (o0a, o0b))
+
+        def cast(g, j, cols):
+            f8, o0s = outs[g]
+            nc.scalar.activation(
+                out=f8[:, j, cols], in_=o0s[j // 2][:, j % 2, cols], func=COPY, scale=Y_SCALE, saturate=False
+            )
+
+        def multiply(g, j, halves, cast_each_half):
+            xc, xs = x_codes[g]
+            o0 = outs[g][1][j // 2]
+            for h in halves:
+                acc = psum.tile([P, HALF], F32, name="acc", tag="bank")
+                for c in range(PASSES):
+                    nc.tensor.matmul_mx(
+                        out=acc[:],
+                        lhsT=xc[:, j, c, :].bitcast(FP8X4),
+                        lhsT_scale=xs[:, j, c, :],
+                        rhs=w_codes[:, h, c, :].bitcast(FP8X4),
+                        rhs_scale=w_scales[:, h, c, :],
+                        start=(c == 0),
+                        stop=(c == PASSES - 1),
                     )
-                nc.sync.dma_start(out=o0_view[g][:, 2 * a : 2 * a + 2, :], in_=o0[:])
-            nc.sync.dma_start(out=o1_view[g], in_=f8[:].rearrange("p j n -> p (j n)").bitcast(U8))
+                cols = slice(HALF * h, HALF * (h + 1))
+                nc.vector.tensor_tensor(out=o0[:, j % 2, cols], in0=acc[:], in1=bias[:, cols], op=ADD)
+                if cast_each_half:
+                    cast(g, j, cols)
+
+        def finish(g, j):
+            f8, o0s = outs[g]
+            chunks0, chunks1 = store_chunks(g)
+            for j0, nj in chunks0:
+                if j0 + nj - 1 == j:
+                    nc.sync.dma_start(
+                        out=o0_view[g][:, j0 : j0 + nj, :], in_=o0s[j0 // 2][:, j0 % 2 : j0 % 2 + nj, :]
+                    )
+            for j0, nj in chunks1:
+                if j0 + nj - 1 == j:
+                    nc.sync.dma_start(
+                        out=o1_view[g][:, N * j0 : N * (j0 + nj)],
+                        in_=f8[:, j0 : j0 + nj, :].rearrange("p j n -> p (j n)").bitcast(U8),
+                    )
 
         warm(WARM_FIRST)
-        prepare_w(0)
+        prepare_w(0, True)
         transpose_x(0, (1, 3), True)
         for h in range(HALVES):
             bp = psum.tile([P, HALF], F32, name="bp", tag="bank")
@@ -187,9 +215,27 @@ def tile_groupfc_kernel(tc, data, W, b, out_0, out_1):
                 nc.vector.tensor_copy(out=bias[:, cols], in_=bp[:])
             else:
                 nc.scalar.copy(out=bias[:, cols], in_=bp[:])
-        prepare_w(1)
-        for g in range(GROUPS):
-            quantise_x(g)
+        quantise_x(0)
+        prepare_w(1, False)
+        open_group(0)
+        for j in range(J):
+            multiply(0, j, (0,), False)
+        transpose_x(1, (3,), False)
+        for j in range(J):
+            multiply(0, j, (1,), False)
+            cast(0, j, slice(0, N))
+            finish(0, j)
+            if j == 1:
+                quantise_x(1)
+        for g in range(1, GROUPS):
             if g + 1 < GROUPS:
                 transpose_x(g + 1, (3,), False)
-            multiply(g)
+            open_group(g)
+            for j in range(J):
+                very_last = g == GROUPS - 1 and j == J - 1
+                multiply(g, j, (0, 1), very_last)
+                if not very_last:
+                    cast(g, j, slice(0, N))
+                finish(g, j)
+                if j == 1 and g + 1 < GROUPS:
+                    quantise_x(g + 1)

@@ -15,6 +15,7 @@ FP8X4 = mybir.dt.float8_e4m3fn_x4
 FP8 = mybir.dt.float8_e4m3fn
 COPY = mybir.ActivationFunctionType.Copy
 ADD = mybir.AluOpType.add
+MULT = mybir.AluOpType.mult
 
 P = 128
 GROUPS = 8
@@ -23,6 +24,7 @@ PASSES = 2
 HALVES = 2
 HALF = 512
 WARM_FIRST = 8
+FIRST_SORTED = 2
 
 
 def tile_groupfc_kernel(tc, data, W, b, out_0, out_1):
@@ -30,6 +32,8 @@ def tile_groupfc_kernel(tc, data, W, b, out_0, out_1):
     with ExitStack() as ctx:
         const = ctx.enter_context(tc.tile_pool(name="const", bufs=1))
         xin = ctx.enter_context(tc.tile_pool(name="xin", bufs=1))
+        xrot = ctx.enter_context(tc.tile_pool(name="xrot", bufs=4))
+        xrp = ctx.enter_context(tc.tile_pool(name="xrp", bufs=3))
         xgp = ctx.enter_context(tc.tile_pool(name="xgp", bufs=4))
         xcp = ctx.enter_context(tc.tile_pool(name="xcp", bufs=2))
         o0p = ctx.enter_context(tc.tile_pool(name="o0p", bufs=8))
@@ -67,10 +71,30 @@ def tile_groupfc_kernel(tc, data, W, b, out_0, out_1):
             )
 
         def load_x(g, j0, nj):
-            t = xin.tile([P, nj, K], BF16, name="x%d_%d" % (g, j0), tag="x%d_%d" % (g, j0))
+            if g < FIRST_SORTED:
+                t = xin.tile([P, nj, K], BF16, name="x%d_%d" % (g, j0), tag="x%d_%d" % (g, j0))
+            else:
+                t = xrot.tile([P, nj, K], BF16, name="xq", tag="xq")
             nc.sync.dma_start(out=t[:], in_=x_view[g][:, j0 : j0 + nj, :])
             for j in range(nj):
                 x_tiles[(g, j0 + j)] = t[:, j, :]
+
+        x_sorted = {}
+
+        def sort_words(g):
+            xr = xrp.tile([P, J, 2, K // 2], BF16, name="xr", tag="xr")
+            x_sorted[g] = xr
+            for j in range(J):
+                src = x_tiles[(g, j)].rearrange("p (q u e) -> p u q e", u=2, e=2)
+                for u in range(2):
+                    nc.gpsimd.tensor_scalar(
+                        out=xr[:, j, u, :].rearrange("p (q e) -> p q e", e=2),
+                        in0=src[:, u],
+                        scalar1=1.0,
+                        scalar2=0.0,
+                        op0=MULT,
+                        op1=ADD,
+                    )
 
         load_w(0)
         load_w(1)
@@ -79,8 +103,10 @@ def tile_groupfc_kernel(tc, data, W, b, out_0, out_1):
         nc.sync.dma_start(out=brow[0:1, :], in_=b.rearrange("(o n) -> o n", o=1))
         load_w(2)
         load_w(3)
-        for g in range(1, GROUPS):
+        for g in range(1, FIRST_SORTED + 4):
             load_x(g, 0, J)
+        for g in range(FIRST_SORTED, FIRST_SORTED + 3):
+            sort_words(g)
 
         def warm(n):
             wp = psum.tile([P, HALF], F32, name="wp", tag="bank")
@@ -95,6 +121,13 @@ def tile_groupfc_kernel(tc, data, W, b, out_0, out_1):
                     nc.tensor.transpose(
                         tp[:, c, u, :], words[:, 256 * c + u : 256 * (c + 1) : 2], ident[:]
                     )
+            return tp
+
+        def transposes_sorted(src):
+            tp = psum.tile([P, PASSES, 2, P], F32, name="tp", tag="bank")
+            for c in range(PASSES):
+                for u in range(2):
+                    nc.tensor.transpose(tp[:, c, u, :], src[:, u, 256 * c : 256 * (c + 1)].bitcast(F32), ident[:])
             return tp
 
         def copy_out(on_vector, dst_words, tp):
@@ -134,7 +167,10 @@ def tile_groupfc_kernel(tc, data, W, b, out_0, out_1):
                 x_grouped[(g, a)] = xg
                 for jj in range(2):
                     j = 2 * a + jj
-                    tp = transposes(x_tiles[(g, j)])
+                    if g < FIRST_SORTED:
+                        tp = transposes(x_tiles[(g, j)])
+                    else:
+                        tp = transposes_sorted(x_sorted[g][:, j])
                     if warm_each:
                         warm(1)
                     copy_out(j in vector_js, xg[:, jj].bitcast(F32), tp)
@@ -227,9 +263,12 @@ def tile_groupfc_kernel(tc, data, W, b, out_0, out_1):
             finish(0, j)
             if j == 1:
                 quantise_x(1)
+        load_x(FIRST_SORTED + 4, 0, J)
         for g in range(1, GROUPS):
             if g + 1 < GROUPS:
                 transpose_x(g + 1, (3,), False)
+            if FIRST_SORTED <= g + 1 and g + 4 < GROUPS:
+                sort_words(g + 4)
             open_group(g)
             for j in range(J):
                 very_last = g == GROUPS - 1 and j == J - 1
@@ -239,3 +278,5 @@ def tile_groupfc_kernel(tc, data, W, b, out_0, out_1):
                 finish(g, j)
                 if j == 1 and g + 1 < GROUPS:
                     quantise_x(g + 1)
+            if g == 1:
+                load_x(FIRST_SORTED + 5, 0, J)

@@ -15,7 +15,6 @@ FP8X4 = mybir.dt.float8_e4m3fn_x4
 FP8 = mybir.dt.float8_e4m3fn
 COPY = mybir.ActivationFunctionType.Copy
 ADD = mybir.AluOpType.add
-MULT = mybir.AluOpType.mult
 
 P = 128
 GROUPS = 8
@@ -24,7 +23,7 @@ PASSES = 2
 HALVES = 2
 HALF = 512
 WARM_FIRST = 8
-FIRST_SORTED = 2
+FIRST_FINE = 5
 
 
 def tile_groupfc_kernel(tc, data, W, b, out_0, out_1):
@@ -32,11 +31,9 @@ def tile_groupfc_kernel(tc, data, W, b, out_0, out_1):
     with ExitStack() as ctx:
         const = ctx.enter_context(tc.tile_pool(name="const", bufs=1))
         xin = ctx.enter_context(tc.tile_pool(name="xin", bufs=1))
-        xrot = ctx.enter_context(tc.tile_pool(name="xrot", bufs=4))
-        xrp = ctx.enter_context(tc.tile_pool(name="xrp", bufs=3))
         xgp = ctx.enter_context(tc.tile_pool(name="xgp", bufs=4))
         xcp = ctx.enter_context(tc.tile_pool(name="xcp", bufs=2))
-        o0p = ctx.enter_context(tc.tile_pool(name="o0p", bufs=8))
+        o0p = ctx.enter_context(tc.tile_pool(name="o0p", bufs=7))
         o1p = ctx.enter_context(tc.tile_pool(name="o1p", bufs=4))
         psum = ctx.enter_context(tc.psum_pool(name="psum", bufs=8))
         ctx.enter_context(tc.manual_schedule())
@@ -63,6 +60,7 @@ def tile_groupfc_kernel(tc, data, W, b, out_0, out_1):
         for q in range(4):
             w_raw.append(const.tile([P, 2, K], BF16, name="w_raw%d" % q, tag="w_raw%d" % q))
         x_tiles = {}
+        x_loaded = {}
 
         def load_w(q):
             nc.sync.dma_start(
@@ -71,30 +69,11 @@ def tile_groupfc_kernel(tc, data, W, b, out_0, out_1):
             )
 
         def load_x(g, j0, nj):
-            if g < FIRST_SORTED:
-                t = xin.tile([P, nj, K], BF16, name="x%d_%d" % (g, j0), tag="x%d_%d" % (g, j0))
-            else:
-                t = xrot.tile([P, nj, K], BF16, name="xq", tag="xq")
+            t = xin.tile([P, nj, K], BF16, name="x%d_%d" % (g, j0), tag="x%d_%d" % (g, j0))
             nc.sync.dma_start(out=t[:], in_=x_view[g][:, j0 : j0 + nj, :])
+            x_loaded[(g, j0)] = t
             for j in range(nj):
                 x_tiles[(g, j0 + j)] = t[:, j, :]
-
-        x_sorted = {}
-
-        def sort_words(g):
-            xr = xrp.tile([P, J, 2, K // 2], BF16, name="xr", tag="xr")
-            x_sorted[g] = xr
-            for j in range(J):
-                src = x_tiles[(g, j)].rearrange("p (q u e) -> p u q e", u=2, e=2)
-                for u in range(2):
-                    nc.gpsimd.tensor_scalar(
-                        out=xr[:, j, u, :].rearrange("p (q e) -> p q e", e=2),
-                        in0=src[:, u],
-                        scalar1=1.0,
-                        scalar2=0.0,
-                        op0=MULT,
-                        op1=ADD,
-                    )
 
         load_w(0)
         load_w(1)
@@ -103,10 +82,8 @@ def tile_groupfc_kernel(tc, data, W, b, out_0, out_1):
         nc.sync.dma_start(out=brow[0:1, :], in_=b.rearrange("(o n) -> o n", o=1))
         load_w(2)
         load_w(3)
-        for g in range(1, FIRST_SORTED + 4):
+        for g in range(1, GROUPS):
             load_x(g, 0, J)
-        for g in range(FIRST_SORTED, FIRST_SORTED + 3):
-            sort_words(g)
 
         def warm(n):
             wp = psum.tile([P, HALF], F32, name="wp", tag="bank")
@@ -122,6 +99,13 @@ def tile_groupfc_kernel(tc, data, W, b, out_0, out_1):
                         tp[:, c, u, :], words[:, 256 * c + u : 256 * (c + 1) : 2], ident[:]
                     )
             return tp
+
+        def sort_words(name, src):
+            dst = const.tile([P, 2, 2, K // 2], BF16, name=name, tag=name)
+            nc.vector.tensor_copy(
+                out=dst[:].bitcast(F32), in_=src.bitcast(F32).rearrange("p n (q u) -> p n u q", u=2)
+            )
+            return dst
 
         def transposes_sorted(src):
             tp = psum.tile([P, PASSES, 2, P], F32, name="tp", tag="bank")
@@ -145,13 +129,15 @@ def tile_groupfc_kernel(tc, data, W, b, out_0, out_1):
         w_codes = const.tile([P, HALVES, PASSES, HALF], U32, name="w_codes", tag="w_codes", align_bytes=64)
         w_scales = const.tile([P, HALVES, PASSES, HALF], U8, name="w_scales", tag="w_scales", align_bytes=64)
 
-        def prepare_w(h, warm_each):
-            for rr in range(4):
-                r = 4 * h + rr
+        def prepare_w(r, on_vector, sorted_src):
+            h, rr = r // 4, r % 4
+            if sorted_src is None:
                 tp = transposes(w_raw[r // 2][:, r % 2, :])
-                if warm_each:
-                    warm(1)
-                copy_out(rr % 2 == 0, w_grouped[h][:, :, P * rr : P * (rr + 1), :].bitcast(F32), tp)
+            else:
+                tp = transposes_sorted(sorted_src[:, r % 2])
+            copy_out(on_vector, w_grouped[h][:, :, P * rr : P * (rr + 1), :].bitcast(F32), tp)
+
+        def quantise_w(h):
             nc.vector.quantize_mx(
                 out=w_codes[:, h].rearrange("p c n -> p (c n)").bitcast(FP8X4),
                 scales=w_scales[:, h].rearrange("p c n -> p (c n)"),
@@ -161,36 +147,44 @@ def tile_groupfc_kernel(tc, data, W, b, out_0, out_1):
         x_grouped = {}
         x_codes = {}
 
-        def transpose_x(g, vector_js, warm_each):
+        def transpose_pair(g, a, vector_js, sorted_src):
+            xg = xgp.tile([P, 2, PASSES, P, 4], BF16, name="xg", tag="xg", align_bytes=64)
+            x_grouped[(g, a)] = xg
+            for jj in range(2):
+                j = 2 * a + jj
+                if sorted_src is None:
+                    tp = transposes(x_tiles[(g, j)])
+                else:
+                    tp = transposes_sorted(sorted_src[:, jj])
+                copy_out(j in vector_js, xg[:, jj].bitcast(F32), tp)
+
+        def transpose_x(g, vector_js):
             for a in range(2):
-                xg = xgp.tile([P, 2, PASSES, P, 4], BF16, name="xg", tag="xg", align_bytes=64)
-                x_grouped[(g, a)] = xg
-                for jj in range(2):
-                    j = 2 * a + jj
-                    if g < FIRST_SORTED:
-                        tp = transposes(x_tiles[(g, j)])
-                    else:
-                        tp = transposes_sorted(x_sorted[g][:, j])
-                    if warm_each:
-                        warm(1)
-                    copy_out(j in vector_js, xg[:, jj].bitcast(F32), tp)
+                transpose_pair(g, a, vector_js, None)
+
+        def quantise_pair(g, a):
+            if a == 0:
+                xc = xcp.tile([P, J, PASSES, P], U32, name="xc", tag="xc", align_bytes=64)
+                xs = xcp.tile([P, J, PASSES, P], U8, name="xs", tag="xs", align_bytes=64)
+                x_codes[g] = (xc, xs)
+            xc, xs = x_codes[g]
+            nc.vector.quantize_mx(
+                out=xc[:, 2 * a : 2 * a + 2].rearrange("p j c r -> p (j c r)").bitcast(FP8X4),
+                scales=xs[:, 2 * a : 2 * a + 2].rearrange("p j c r -> p (j c r)"),
+                in_=x_grouped[(g, a)][:].rearrange("p j c r t -> p (j c r t)"),
+            )
 
         def quantise_x(g):
-            xc = xcp.tile([P, J, PASSES, P], U32, name="xc", tag="xc", align_bytes=64)
-            xs = xcp.tile([P, J, PASSES, P], U8, name="xs", tag="xs", align_bytes=64)
-            x_codes[g] = (xc, xs)
             for a in range(2):
-                nc.vector.quantize_mx(
-                    out=xc[:, 2 * a : 2 * a + 2].rearrange("p j c r -> p (j c r)").bitcast(FP8X4),
-                    scales=xs[:, 2 * a : 2 * a + 2].rearrange("p j c r -> p (j c r)"),
-                    in_=x_grouped[(g, a)][:].rearrange("p j c r t -> p (j c r t)"),
-                )
+                quantise_pair(g, a)
 
         outs = {}
 
         def store_chunks(g):
             if g == GROUPS - 1:
-                return ((0, 2), (2, 1), (3, 1)), ((0, 2), (2, 1), (3, 1))
+                return ((0, 1), (1, 1), (2, 1), (3, 1)), ((0, 2), (2, 1), (3, 1))
+            if g >= FIRST_FINE:
+                return ((0, 1), (1, 1), (2, 1), (3, 1)), ((0, 2), (2, 2))
             return ((0, 2), (2, 2)), ((0, 4),)
 
         def open_group(g):
@@ -241,8 +235,15 @@ def tile_groupfc_kernel(tc, data, W, b, out_0, out_1):
                     )
 
         warm(WARM_FIRST)
-        prepare_w(0, True)
-        transpose_x(0, (1, 3), True)
+        for q in range(2):
+            ws = sort_words("ws%d" % q, w_raw[q][:])
+            prepare_w(2 * q, False, ws)
+            prepare_w(2 * q + 1, False, ws)
+        xs0 = sort_words("xs0", x_loaded[(0, 0)][:])
+        transpose_pair(0, 0, (), xs0)
+        xs1 = sort_words("xs1", x_loaded[(0, 2)][:])
+        quantise_w(0)
+        transpose_pair(0, 1, (), xs1)
         for h in range(HALVES):
             bp = psum.tile([P, HALF], F32, name="bp", tag="bank")
             cols = slice(HALF * h, HALF * (h + 1))
@@ -251,24 +252,26 @@ def tile_groupfc_kernel(tc, data, W, b, out_0, out_1):
                 nc.vector.tensor_copy(out=bias[:, cols], in_=bp[:])
             else:
                 nc.scalar.copy(out=bias[:, cols], in_=bp[:])
-        quantise_x(0)
-        prepare_w(1, False)
+        quantise_pair(0, 0)
+        prepare_w(4, True, None)
+        prepare_w(5, False, None)
+        quantise_pair(0, 1)
+        prepare_w(6, True, None)
+        prepare_w(7, False, None)
+        quantise_w(1)
         open_group(0)
         for j in range(J):
             multiply(0, j, (0,), False)
-        transpose_x(1, (3,), False)
+        transpose_x(1, (3,))
         for j in range(J):
             multiply(0, j, (1,), False)
             cast(0, j, slice(0, N))
             finish(0, j)
             if j == 1:
                 quantise_x(1)
-        load_x(FIRST_SORTED + 4, 0, J)
         for g in range(1, GROUPS):
             if g + 1 < GROUPS:
-                transpose_x(g + 1, (3,), False)
-            if FIRST_SORTED <= g + 1 and g + 4 < GROUPS:
-                sort_words(g + 4)
+                transpose_x(g + 1, (3,))
             open_group(g)
             for j in range(J):
                 very_last = g == GROUPS - 1 and j == J - 1
@@ -278,5 +281,3 @@ def tile_groupfc_kernel(tc, data, W, b, out_0, out_1):
                 finish(g, j)
                 if j == 1 and g + 1 < GROUPS:
                     quantise_x(g + 1)
-            if g == 1:
-                load_x(FIRST_SORTED + 5, 0, J)

@@ -31,7 +31,8 @@ def tile_groupfc_kernel(tc, data, W, b, out_0, out_1):
     with ExitStack() as ctx:
         const = ctx.enter_context(tc.tile_pool(name="const", bufs=1))
         xin = ctx.enter_context(tc.tile_pool(name="xin", bufs=1))
-        xgp = ctx.enter_context(tc.tile_pool(name="xgp", bufs=4))
+        srt = ctx.enter_context(tc.tile_pool(name="srt", bufs=4))
+        xgp = ctx.enter_context(tc.tile_pool(name="xgp", bufs=2))
         xcp = ctx.enter_context(tc.tile_pool(name="xcp", bufs=2))
         o0p = ctx.enter_context(tc.tile_pool(name="o0p", bufs=7))
         o1p = ctx.enter_context(tc.tile_pool(name="o1p", bufs=4))
@@ -100,11 +101,13 @@ def tile_groupfc_kernel(tc, data, W, b, out_0, out_1):
                     )
             return tp
 
-        def sort_words(name, src):
-            dst = const.tile([P, 2, 2, K // 2], BF16, name=name, tag=name)
-            nc.vector.tensor_copy(
-                out=dst[:].bitcast(F32), in_=src.bitcast(F32).rearrange("p n (q u) -> p n u q", u=2)
-            )
+        def sort_words(on_vector, src):
+            dst = srt.tile([P, src.shape[1], 2, K // 2], BF16, name="sorted", tag="sorted")
+            words = src.bitcast(F32).rearrange("p n (q u) -> p n u q", u=2)
+            if on_vector:
+                nc.vector.tensor_copy(out=dst[:].bitcast(F32), in_=words)
+            else:
+                nc.scalar.copy(out=dst[:].bitcast(F32), in_=words)
             return dst
 
         def transposes_sorted(src):
@@ -147,36 +150,38 @@ def tile_groupfc_kernel(tc, data, W, b, out_0, out_1):
         x_grouped = {}
         x_codes = {}
 
-        def transpose_pair(g, a, vector_js, sorted_src):
-            xg = xgp.tile([P, 2, PASSES, P, 4], BF16, name="xg", tag="xg", align_bytes=64)
-            x_grouped[(g, a)] = xg
-            for jj in range(2):
-                j = 2 * a + jj
-                if sorted_src is None:
-                    tp = transposes(x_tiles[(g, j)])
+        x_sorted = {}
+
+        def transpose_tiles(g, js, vector_js):
+            if js[0] == 0:
+                xg = xgp.tile([P, J, PASSES, P, 4], BF16, name="xg", tag="xg", align_bytes=64)
+                x_grouped[g] = xg
+            xg = x_grouped[g]
+            for j in js:
+                if (g, j) in x_sorted:
+                    tp = transposes_sorted(x_sorted[(g, j)])
                 else:
-                    tp = transposes_sorted(sorted_src[:, jj])
-                copy_out(j in vector_js, xg[:, jj].bitcast(F32), tp)
+                    tp = transposes(x_tiles[(g, j)])
+                copy_out(j in vector_js, xg[:, j].bitcast(F32), tp)
 
         def transpose_x(g, vector_js):
-            for a in range(2):
-                transpose_pair(g, a, vector_js, None)
+            transpose_tiles(g, (0, 1, 2, 3), vector_js)
 
-        def quantise_pair(g, a):
-            if a == 0:
+        def quantise_tiles(g, j0, nj):
+            if j0 == 0:
                 xc = xcp.tile([P, J, PASSES, P], U32, name="xc", tag="xc", align_bytes=64)
                 xs = xcp.tile([P, J, PASSES, P], U8, name="xs", tag="xs", align_bytes=64)
                 x_codes[g] = (xc, xs)
             xc, xs = x_codes[g]
             nc.vector.quantize_mx(
-                out=xc[:, 2 * a : 2 * a + 2].rearrange("p j c r -> p (j c r)").bitcast(FP8X4),
-                scales=xs[:, 2 * a : 2 * a + 2].rearrange("p j c r -> p (j c r)"),
-                in_=x_grouped[(g, a)][:].rearrange("p j c r t -> p (j c r t)"),
+                out=xc[:, j0 : j0 + nj].rearrange("p j c r -> p (j c r)").bitcast(FP8X4),
+                scales=xs[:, j0 : j0 + nj].rearrange("p j c r -> p (j c r)"),
+                in_=x_grouped[g][:, j0 : j0 + nj].rearrange("p j c r t -> p (j c r t)"),
             )
 
         def quantise_x(g):
-            for a in range(2):
-                quantise_pair(g, a)
+            quantise_tiles(g, 0, 2)
+            quantise_tiles(g, 2, 2)
 
         outs = {}
 
@@ -236,14 +241,17 @@ def tile_groupfc_kernel(tc, data, W, b, out_0, out_1):
 
         warm(WARM_FIRST)
         for q in range(2):
-            ws = sort_words("ws%d" % q, w_raw[q][:])
+            ws = sort_words(True, w_raw[q][:])
             prepare_w(2 * q, False, ws)
             prepare_w(2 * q + 1, False, ws)
-        xs0 = sort_words("xs0", x_loaded[(0, 0)][:])
-        transpose_pair(0, 0, (), xs0)
-        xs1 = sort_words("xs1", x_loaded[(0, 2)][:])
+        for a in range(2):
+            pair = sort_words(True, x_loaded[(0, 2 * a)][:])
+            x_sorted[(0, 2 * a)] = pair[:, 0]
+            x_sorted[(0, 2 * a + 1)] = pair[:, 1]
+            if a == 0:
+                transpose_tiles(0, (0, 1), ())
         quantise_w(0)
-        transpose_pair(0, 1, (), xs1)
+        transpose_tiles(0, (2, 3), ())
         for h in range(HALVES):
             bp = psum.tile([P, HALF], F32, name="bp", tag="bank")
             cols = slice(HALF * h, HALF * (h + 1))
@@ -252,13 +260,15 @@ def tile_groupfc_kernel(tc, data, W, b, out_0, out_1):
                 nc.vector.tensor_copy(out=bias[:, cols], in_=bp[:])
             else:
                 nc.scalar.copy(out=bias[:, cols], in_=bp[:])
-        quantise_pair(0, 0)
+        quantise_tiles(0, 0, 2)
         prepare_w(4, True, None)
         prepare_w(5, False, None)
-        quantise_pair(0, 1)
+        quantise_tiles(0, 2, 2)
         prepare_w(6, True, None)
         prepare_w(7, False, None)
         quantise_w(1)
+        for j in range(J):
+            x_sorted[(1, j)] = sort_words(False, x_loaded[(1, 0)][:, j : j + 1, :])[:, 0]
         open_group(0)
         for j in range(J):
             multiply(0, j, (0,), False)

from contextlib import ExitStack

import concourse.mybir as mybir
from concourse.masks import make_identity

TOKENS, K, N = 4096, 1024, 1024
FLOPS = 2 * TOKENS * K * N
Y_SCALE = 340.0

F32 = mybir.dt.float32
BF16 = mybir.dt.bfloat16
U32 = mybir.dt.uint32
U8 = mybir.dt.uint8
FP8X4 = mybir.dt.float8_e4m3fn_x4
FP8 = mybir.dt.float8_e4m3fn
COPY = mybir.ActivationFunctionType.Copy
ADD = mybir.AluOpType.add

P = 128
GROUPS = 8
J = 4
PASSES = 2
HALVES = 2
HALF = 512
WARM_FIRST = 8
FIRST_FINE = 5


def tile_groupfc_kernel(tc, data, W, b, out_0, out_1):
    nc = tc.nc
    with ExitStack() as ctx:
        const = ctx.enter_context(tc.tile_pool(name="const", bufs=1))
        xin = ctx.enter_context(tc.tile_pool(name="xin", bufs=1))
        srt = ctx.enter_context(tc.tile_pool(name="srt", bufs=4))
        xgp = ctx.enter_context(tc.tile_pool(name="xgp", bufs=2))
        xcp = ctx.enter_context(tc.tile_pool(name="xcp", bufs=2))
        o0p = ctx.enter_context(tc.tile_pool(name="o0p", bufs=7))
        o1p = ctx.enter_context(tc.tile_pool(name="o1p", bufs=4))
        psum = ctx.enter_context(tc.psum_pool(name="psum", bufs=8))
        ctx.enter_context(tc.manual_schedule())

        x_view = data.rearrange("(g p j) k -> g p j k", p=P, j=J)
        o0_view = out_0.rearrange("(g p j) n -> g p j n", p=P, j=J)
        o1_view = out_1.rearrange("(g p j) n -> g p (j n)", p=P, j=J)

        ones = const.tile([P, P], BF16, name="ones", tag="ones")
        nc.vector.memset(ones[:], 1.0)
        zeros = const.tile([P, HALF], BF16, name="zeros", tag="zeros")
        nc.vector.memset(zeros[:], 0.0)
        brow = const.tile([P, N], BF16, name="brow", tag="brow")
        nc.vector.memset(brow[:], 0.0)
        tiny = const.tile([P, 1], F32, name="tiny", tag="tiny")
        nc.vector.memset(tiny[:], 0.0)
        tiny2 = const.tile([P, 1], F32, name="tiny2", tag="tiny2")
        nc.scalar.activation(out=tiny2[:], in_=tiny[:], func=COPY, scale=Y_SCALE)
        ident = const.tile([P, P], F32, name="ident", tag="ident")
        make_identity(nc, ident[:])
        bias = const.tile([P, N], F32, name="bias", tag="bias")

        w_raw = []
        for q in range(4):
            w_raw.append(const.tile([P, 2, K], BF16, name="w_raw%d" % q, tag="w_raw%d" % q))
        x_tiles = {}
        x_loaded = {}

        def load_w(q):
            nc.sync.dma_start(
                out=w_raw[q][:],
                in_=W[256 * q : 256 * (q + 1), :].rearrange("(r p) k -> p r k", p=P),
            )

        def load_x(g, j0, nj):
            t = xin.tile([P, nj, K], BF16, name="x%d_%d" % (g, j0), tag="x%d_%d" % (g, j0))
            nc.sync.dma_start(out=t[:], in_=x_view[g][:, j0 : j0 + nj, :])
            x_loaded[(g, j0)] = t
            for j in range(nj):
                x_tiles[(g, j0 + j)] = t[:, j, :]

        load_w(0)
        load_w(1)
        load_x(0, 0, 2)
        load_x(0, 2, 2)
        nc.sync.dma_start(out=brow[0:1, :], in_=b.rearrange("(o n) -> o n", o=1))
        load_w(2)
        load_w(3)
        for g in range(1, GROUPS):
            load_x(g, 0, J)

        def warm(n):
            wp = psum.tile([P, HALF], F32, name="wp", tag="bank")
            for i in range(n):
                nc.tensor.matmul(out=wp[:], lhsT=ones[:], rhs=zeros[:], start=True, stop=True)

        def transposes(src):
            words = src.bitcast(F32)
            tp = psum.tile([P, PASSES, 2, P], F32, name="tp", tag="bank")
            for c in range(PASSES):
                for u in range(2):
                    nc.tensor.transpose(
                        tp[:, c, u, :], words[:, 256 * c + u : 256 * (c + 1) : 2], ident[:]
                    )
            return tp

        def sort_words(on_vector, src):
            dst = srt.tile([P, src.shape[1], 2, K // 2], BF16, name="sorted", tag="sorted")
            words = src.bitcast(F32).rearrange("p n (q u) -> p n u q", u=2)
            if on_vector:
                nc.vector.tensor_copy(out=dst[:].bitcast(F32), in_=words)
            else:
                nc.scalar.copy(out=dst[:].bitcast(F32), in_=words)
            return dst

        def transposes_sorted(src):
            tp = psum.tile([P, PASSES, 2, P], F32, name="tp", tag="bank")
            for c in range(PASSES):
                for u in range(2):
                    nc.tensor.transpose(tp[:, c, u, :], src[:, u, 256 * c : 256 * (c + 1)].bitcast(F32), ident[:])
            return tp

        def copy_out(on_vector, dst_words, tp):
            src = tp[:].rearrange("p c u r -> p c r u")
            if on_vector:
                nc.vector.tensor_copy(out=dst_words, in_=src)
            else:
                nc.scalar.copy(out=dst_words, in_=src)

        w_grouped = []
        for h in range(HALVES):
            w_grouped.append(
                const.tile([P, PASSES, HALF, 4], BF16, name="wg%d" % h, tag="wg%d" % h, align_bytes=64)
            )
        w_codes = const.tile([P, HALVES, PASSES, HALF], U32, name="w_codes", tag="w_codes", align_bytes=64)
        w_scales = const.tile([P, HALVES, PASSES, HALF], U8, name="w_scales", tag="w_scales", align_bytes=64)

        def prepare_w(r, on_vector, sorted_src):
            h, rr = r // 4, r % 4
            if sorted_src is None:
                tp = transposes(w_raw[r // 2][:, r % 2, :])
            else:
                tp = transposes_sorted(sorted_src[:, r % 2])
            copy_out(on_vector, w_grouped[h][:, :, P * rr : P * (rr + 1), :].bitcast(F32), tp)

        def quantise_w(h):
            nc.vector.quantize_mx(
                out=w_codes[:, h].rearrange("p c n -> p (c n)").bitcast(FP8X4),
                scales=w_scales[:, h].rearrange("p c n -> p (c n)"),
                in_=w_grouped[h][:].rearrange("p c n t -> p (c n t)"),
            )

        x_grouped = {}
        x_codes = {}

        x_sorted = {}

        def transpose_tiles(g, js, vector_js):
            if js[0] == 0:
                xg = xgp.tile([P, J, PASSES, P, 4], BF16, name="xg", tag="xg", align_bytes=64)
                x_grouped[g] = xg
            xg = x_grouped[g]
            for j in js:
                if (g, j) in x_sorted:
                    tp = transposes_sorted(x_sorted[(g, j)])
                else:
                    tp = transposes(x_tiles[(g, j)])
                copy_out(j in vector_js, xg[:, j].bitcast(F32), tp)

        def transpose_x(g, vector_js):
            transpose_tiles(g, (0, 1, 2, 3), vector_js)

        def quantise_tiles(g, j0, nj):
            if j0 == 0:
                xc = xcp.tile([P, J, PASSES, P], U32, name="xc", tag="xc", align_bytes=64)
                xs = xcp.tile([P, J, PASSES, P], U8, name="xs", tag="xs", align_bytes=64)
                x_codes[g] = (xc, xs)
            xc, xs = x_codes[g]
            nc.vector.quantize_mx(
                out=xc[:, j0 : j0 + nj].rearrange("p j c r -> p (j c r)").bitcast(FP8X4),
                scales=xs[:, j0 : j0 + nj].rearrange("p j c r -> p (j c r)"),
                in_=x_grouped[g][:, j0 : j0 + nj].rearrange("p j c r t -> p (j c r t)"),
            )

        def quantise_x(g):
            quantise_tiles(g, 0, 2)
            quantise_tiles(g, 2, 2)

        outs = {}

        def store_chunks(g):
            if g == GROUPS - 1:
                return ((0, 1), (1, 1), (2, 1), (3, 1)), ((0, 2), (2, 1), (3, 1))
            if g >= FIRST_FINE:
                return ((0, 1), (1, 1), (2, 1), (3, 1)), ((0, 2), (2, 2))
            return ((0, 2), (2, 2)), ((0, 4),)

        def open_group(g):
            f8 = o1p.tile([P, J, N], FP8, name="f8", tag="f8")
            o0a = o0p.tile([P, 2, N], F32, name="o0", tag="o0")
            o0b = o0p.tile([P, 2, N], F32, name="o0", tag="o0")
            outs[g] = (f8, (o0a, o0b))

        def cast(g, j, cols):
            f8, o0s = outs[g]
            nc.scalar.activation(
                out=f8[:, j, cols], in_=o0s[j // 2][:, j % 2, cols], func=COPY, scale=Y_SCALE, saturate=False
            )

        def multiply(g, j, halves, cast_each_half):
            xc, xs = x_codes[g]
            o0 = outs[g][1][j // 2]
            for h in halves:
                acc = psum.tile([P, HALF], F32, name="acc", tag="bank")
                for c in range(PASSES):
                    nc.tensor.matmul_mx(
                        out=acc[:],
                        lhsT=xc[:, j, c, :].bitcast(FP8X4),
                        lhsT_scale=xs[:, j, c, :],
                        rhs=w_codes[:, h, c, :].bitcast(FP8X4),
                        rhs_scale=w_scales[:, h, c, :],
                        start=(c == 0),
                        stop=(c == PASSES - 1),
                    )
                cols = slice(HALF * h, HALF * (h + 1))
                nc.vector.tensor_tensor(out=o0[:, j % 2, cols], in0=acc[:], in1=bias[:, cols], op=ADD)
                if cast_each_half:
                    cast(g, j, cols)

        def finish(g, j):
            f8, o0s = outs[g]
            chunks0, chunks1 = store_chunks(g)
            for j0, nj in chunks0:
                if j0 + nj - 1 == j:
                    nc.sync.dma_start(
                        out=o0_view[g][:, j0 : j0 + nj, :], in_=o0s[j0 // 2][:, j0 % 2 : j0 % 2 + nj, :]
                    )
            for j0, nj in chunks1:
                if j0 + nj - 1 == j:
                    nc.sync.dma_start(
                        out=o1_view[g][:, N * j0 : N * (j0 + nj)],
                        in_=f8[:, j0 : j0 + nj, :].rearrange("p j n -> p (j n)").bitcast(U8),
                    )

        warm(WARM_FIRST)
        for q in range(2):
            ws = sort_words(True, w_raw[q][:])
            prepare_w(2 * q, False, ws)
            prepare_w(2 * q + 1, False, ws)
        for a in range(2):
            pair = sort_words(True, x_loaded[(0, 2 * a)][:])
            x_sorted[(0, 2 * a)] = pair[:, 0]
            x_sorted[(0, 2 * a + 1)] = pair[:, 1]
            if a == 0:
                transpose_tiles(0, (0, 1), ())
        quantise_w(0)
        transpose_tiles(0, (2, 3), ())
        for h in range(HALVES):
            bp = psum.tile([P, HALF], F32, name="bp", tag="bank")
            cols = slice(HALF * h, HALF * (h + 1))
            nc.tensor.matmul(out=bp[:], lhsT=ones[:], rhs=brow[:, cols], start=True, stop=True)
            if h == 0:
                nc.vector.tensor_copy(out=bias[:, cols], in_=bp[:])
            else:
                nc.scalar.copy(out=bias[:, cols], in_=bp[:])
        quantise_tiles(0, 0, 2)
        prepare_w(4, True, None)
        prepare_w(5, False, None)
        quantise_tiles(0, 2, 2)
        prepare_w(6, True, None)
        prepare_w(7, False, None)
        quantise_w(1)
        for j in range(J):
            x_sorted[(1, j)] = sort_words(False, x_loaded[(1, 0)][:, j : j + 1, :])[:, 0]
        open_group(0)
        for j in range(J):
            multiply(0, j, (0,), False)
        transpose_x(1, (3,))
        for j in range(J):
            multiply(0, j, (1,), False)
            cast(0, j, slice(0, N))
            finish(0, j)
            if j == 1:
                quantise_x(1)
        for g in range(1, GROUPS):
            if g + 1 < GROUPS:
                transpose_x(g + 1, (3,))
            open_group(g)
            for j in range(J):
                very_last = g == GROUPS - 1 and j == J - 1
                multiply(g, j, (0, 1), very_last)
                if not very_last:
                    cast(g, j, slice(0, N))
                finish(g, j)
                if j == 1 and g + 1 < GROUPS:
                    quantise_x(g + 1)
